import numpy as np
import ml_dtypes


def mxq(x, axis, fmt="e4m3"):
    dtype, down = {"e4m3": (ml_dtypes.float8_e4m3fn, 7), "e5m2": (ml_dtypes.float8_e5m2, 14)}[fmt]
    v = np.moveaxis(np.asarray(x, np.float32).astype(ml_dtypes.bfloat16).astype(np.float64), axis, -1)
    blocks = v.reshape(v.shape[:-1] + (-1, 32))
    amax = np.abs(blocks).max(-1, keepdims=True)
    byte = np.maximum(np.where(amax > 0, np.frexp(amax)[1] - 1 + 127, 0) - down, 1)
    scale = np.exp2(byte - 127.0)
    codes = (blocks / scale).astype(np.float32).astype(dtype).astype(np.float64)
    return np.moveaxis((codes * scale).reshape(v.shape), -1, axis)


WIDE = False


def mx_kscale(k):
    if not WIDE:
        return np.ones(k)
    levels = np.array([10, -10, 5, -5, 0])
    if k % 512:
        return np.exp2(np.random.permutation(np.resize(levels, k // 32))).repeat(32)
    a = np.empty((k // 512, 16))
    for p in range(k // 512):
        a[p, :8] = np.random.permutation(np.resize(levels, 8))
        for g in range(8):
            far = levels[np.abs(levels - a[p, g]) >= 10]
            a[p, g + 8] = far[np.random.randint(len(far))]
    return np.exp2(a.ravel()).repeat(32)


BF16 = ml_dtypes.bfloat16


def bf(x):
    return np.asarray(x, np.float32).astype(BF16)


def f64(x):
    return np.asarray(x).astype(np.float64)


B, N, D, L = 1, 1024, 512, 512
SEGS = N // L


def draw0():
    s = mx_kscale(D)
    col = np.concatenate([np.full(D, np.sqrt(SEGS)), np.ones(D)])
    return {"x": bf(np.random.standard_normal((B, N, D)) * s),
            "w_kv": bf(np.random.standard_normal((D, D + D)) * col / np.sqrt(D) / s[:, None])}


def core(x, w_kv):
    kv = mxq(f64(x), 2, "e4m3") @ mxq(f64(w_kv), 0, "e4m3")
    k, v = kv[..., :D], kv[..., D:]
    keys_lm = k.reshape(B, L, SEGS, D).mean(axis=2)
    vals_lm = v.reshape(B, L, SEGS, D).mean(axis=2)
    return v, keys_lm, vals_lm


def e4m3fn_bytes(y):
    return np.clip(np.asarray(y, np.float64), -448.0, 448.0).astype(np.float32).astype(ml_dtypes.float8_e4m3fn).view(np.uint8)


def e4m3fn_values(b):
    return np.asarray(b, np.uint8).view(ml_dtypes.float8_e4m3fn).astype(np.float64)


def setup_inputs():
    d = draw0()
    x0 = np.asarray(d['x']).astype(np.float64)
    s = (np.max(np.abs(x0), axis=(0, 1), keepdims=True) / 448.0).astype(np.float32)
    out = {}
    for k, v in d.items():
        if k == 'x':
            out['x_bytes'] = e4m3fn_bytes(x0 / s.astype(np.float64))
            out['x_scale'] = s
        else:
            out[k] = v
    return out


def reference(x_bytes, x_scale, w_kv):
    return core(e4m3fn_values(x_bytes) * x_scale.astype(np.float64), w_kv)

@@ -1,0 +1,210 @@
+from contextlib import ExitStack
+
+import concourse.mybir as mybir
+from concourse.masks import make_identity
+
+FLOPS = 2 * 1024 * 512 * 1024
+
+F32 = mybir.dt.float32
+BF16 = mybir.dt.bfloat16
+U32 = mybir.dt.uint32
+U8 = mybir.dt.uint8
+FP8 = mybir.dt.float8_e4m3fn
+FP8X4 = mybir.dt.float8_e4m3fn_x4
+MULT = mybir.AluOpType.mult
+COPY = mybir.ActivationFunctionType.Copy
+
+P = 128
+D = 512
+GROUPS = 4
+CHUNK = 128
+BANKS = 8
+
+VECTOR = "C01 W10 W12 X0 R1 Q0 X1 Ee0 Q1 X2 C30 Q2 R0 X3 Ek0 Q3 Ee3 Eo3 El3".split()
+SCALAR = "C00 W11 W13 C10 C11 W02 W00 W01 W03 Eo0 El0 Eo1 Ee1 El1 Eo2 Ee2 El2 Ek1 Ek2 Ek3".split()
+TENSOR = "T01 T00 D1 D2 T10 T11 Pe0 Pl00 Po0 Pl01 T21 T20 D0 Po1 Pl10 Pe1 Pl11 T31 T30 Po2 Pe2 Pk00 Pk01 Pl20 Pl21 Pk10 Pk11 Pk20 Pk21 Pe3 Pl30 Po3 Pk30 Pl31 Pk31".split()
+GPSIMD = "C21 C20 C31".split()
+SYNC = "Se0 So0 Sl0 So1 Se1 Sl1 So2 Se2 Sk0 Sl2 Sk1 Sk2 Se3 So3 Sl3 Sk3".split()
+
+
+def needs(op):
+    kind, a = op[0], op[1]
+    if kind == "C":
+        return ["Q" + str(int(a) - 2)] if int(a) >= 2 else []
+    if kind == "T":
+        return ["C" + op[1:]]
+    if kind == "X":
+        return ["T" + a + "0", "T" + a + "1"]
+    if kind == "Q":
+        return ["X" + a]
+    if kind == "R":
+        return ["W" + a + str(c) for c in range(D // CHUNK)]
+    if kind == "D":
+        return ["W1" + a]
+    if kind == "P":
+        j = op[2]
+        first = ["P" + a + j + "0"] if op[3:] == "1" else []
+        return ["Q" + j, "R0" if a == "k" else "R1"] + first
+    if kind == "E":
+        return ["P" + op[1:] + ("1" if a in "lk" else "")]
+    if kind == "S":
+        return ["E" + op[1:]]
+    return []
+
+
+def tile_ammattention_pa_kernel(tc, x_bytes, x_scale, w_kv, out_0, out_1, out_2):
+    nc = tc.nc
+    x_view = x_bytes.rearrange("o (j m e) k -> m (o j) e k", j=GROUPS, m=P, e=2)
+    w_view = w_kv.rearrange("(p t) n -> p t n", t=4)
+    v_view = out_0.rearrange("o (j m e) n -> m (o j) e n", j=GROUPS, m=P, e=2)
+    kl_view = out_1.rearrange("o (j m) n -> m (o j) n", j=GROUPS, m=P)
+    vl_view = out_2.rearrange("o (j m) n -> m (o j) n", j=GROUPS, m=P)
+
+    with ExitStack() as ctx:
+        sb = ctx.enter_context(tc.tile_pool(name="sb", bufs=1))
+        ps = ctx.enter_context(tc.psum_pool(name="ps", bufs=1))
+        ctx.enter_context(tc.manual_schedule())
+
+        scale4 = sb.tile([P, 4], F32, name="scale4")
+        nc.scalar.dma_start(out=scale4[:], in_=x_scale.rearrange("a b (p t) -> p (a b t)", t=4))
+        x_raw = [sb.tile([P, 2, D], U8, name="x_raw%d" % j) for j in range(GROUPS)]
+        w_raw = [sb.tile([P, 4, D], BF16, name="w_raw%d" % h) for h in range(2)]
+        nc.sync.dma_start(out=x_raw[0][:], in_=x_view[:, 0])
+        for c0 in (0, D // 2):
+            nc.sync.dma_start(out=w_raw[1][:, :, c0:c0 + D // 2], in_=w_view[:, :, D + c0:D + c0 + D // 2])
+        for j in range(1, GROUPS):
+            nc.sync.dma_start(out=x_raw[j][:], in_=x_view[:, j])
+        nc.sync.dma_start(out=w_raw[0][:], in_=w_view[:, :, 0:D])
+
+        zeros = sb.tile([P, P], BF16, name="zeros")
+        nc.gpsimd.memset(zeros[:], 0.0)
+        ident = sb.tile([P, P], F32, name="ident")
+        make_identity(nc, ident[:])
+        one_col = sb.tile([P, 1], F32, name="one_col")
+        one_out = sb.tile([P, 1], F32, name="one_out")
+        nc.vector.memset(one_col[:], 0.0)
+        nc.scalar.activation(out=one_out[:], in_=one_col[:], func=COPY, scale=0.5)
+
+        x_grp = [sb.tile([P, 2 * P, 4], BF16, name="x_grp%d" % j, align_bytes=64) for j in range(GROUPS)]
+        x_bf = {}
+        x_codes = [sb.tile([P, 2 * P], U32, name="x_codes%d" % j, align_bytes=64) for j in range(GROUPS)]
+        x_scales = [sb.tile([P, 2 * P], U8, name="x_scales%d" % j, align_bytes=64) for j in range(GROUPS)]
+        w_grp = [sb.tile([P, D, 4], BF16, name="w_grp%d" % h, align_bytes=64) for h in range(2)]
+        w_codes = [sb.tile([P, D], U32, name="w_codes%d" % h, align_bytes=64) for h in range(2)]
+        w_scales = [sb.tile([P, D], U8, name="w_scales%d" % h, align_bytes=64) for h in range(2)]
+        v_sb = [sb.tile([P, 2, D], F32, name="v_sb%d" % j) for j in range(GROUPS)]
+        kl_sb = [sb.tile([P, D], F32, name="kl_sb%d" % j) for j in range(GROUPS)]
+        vl_sb = [sb.tile([P, D], F32, name="vl_sb%d" % j) for j in range(GROUPS)]
+
+        opened = []
+        emptied = set()
+        psum_of = {}
+
+        def result(what, j):
+            if what == "e":
+                return v_sb[j][:, 0, :], v_view[:, j, 0, :]
+            if what == "o":
+                return v_sb[j][:, 1, :], v_view[:, j, 1, :]
+            if what == "l":
+                return vl_sb[j][:], vl_view[:, j]
+            return kl_sb[j][:], kl_view[:, j]
+
+        def emit(op, queue):
+            kind = op[0]
+            on_vector = queue is VECTOR
+            if kind == "C":
+                j, e = int(op[1]), int(op[2])
+                if j not in x_bf:
+                    x_bf[j] = sb.tile([P, 2, D], BF16, name=("x_bf%d" % j) if j < 2 else ("x_grp%d" % (j - 2)), align_bytes=64)
+                if on_vector:
+                    nc.vector.tensor_copy(out=x_bf[j][:, e, :], in_=x_raw[j][:, e, :].bitcast(FP8))
+                elif queue is GPSIMD:
+                    nc.gpsimd.tensor_copy(out=x_bf[j][:, e, :], in_=x_raw[j][:, e, :].bitcast(FP8))
+                else:
+                    nc.scalar.copy(out=x_bf[j][:, e, :], in_=x_raw[j][:, e, :].bitcast(FP8))
+            elif kind == "T":
+                j, e = int(op[1]), int(op[2])
+                words = x_bf[j][:, e, :].bitcast(F32)
+                for u in range(2):
+                    nc.tensor.transpose(psum_of["t" + op[1]][:, u * 2 * P + e * P:u * 2 * P + (e + 1) * P], words[:, u:2 * P:2], ident[:])
+            elif kind == "X":
+                j = int(op[1])
+                nc.vector.tensor_tensor(
+                    out=x_grp[j][:].rearrange("p c (u i) -> p c u i", u=2),
+                    in0=psum_of["t" + op[1]][:].bitcast(BF16).rearrange("p (u c i) -> p c u i", u=2, i=2),
+                    in1=scale4[:].rearrange("p (u i) -> p u i", u=2).unsqueeze(1).to_broadcast([P, 2 * P, 2, 2]),
+                    op=MULT,
+                )
+            elif kind == "Q":
+                j = int(op[1])
+                nc.vector.quantize_mx(out=x_codes[j][:].bitcast(FP8X4), scales=x_scales[j][:], in_=x_grp[j][:].rearrange("p c t -> p (c t)"))
+            elif kind == "W":
+                h, c0 = int(op[1]), int(op[2]) * CHUNK
+                src = w_raw[h][:, :, c0:c0 + CHUNK].rearrange("p t (c i) -> p c t i", i=4)
+                dst = w_grp[h][:, c0:c0 + CHUNK, :].rearrange("p (c i) t -> p c t i", i=4)
+                if on_vector:
+                    nc.vector.tensor_copy(out=dst, in_=src)
+                else:
+                    nc.scalar.copy(out=dst, in_=src)
+            elif kind == "R":
+                h = int(op[1])
+                nc.vector.quantize_mx(out=w_codes[h][:].bitcast(FP8X4), scales=w_scales[h][:], in_=w_grp[h][:].rearrange("p n t -> p (n t)"))
+            elif kind == "D":
+                c0 = int(op[1]) * CHUNK
+                nc.tensor.matmul(out=psum_of["d"][:], lhsT=zeros[:], rhs=w_grp[1][:, c0:c0 + CHUNK, :].rearrange("p n t -> p (n t)"), start=True, stop=True)
+            elif kind == "P":
+                what, j = op[1], int(op[2])
+                e = {"e": 0, "o": 1}.get(what, int(op[3:] or 0))
+                h = 0 if what == "k" else 1
+                nc.tensor.matmul_mx(
+                    out=psum_of[op[1:3]][:],
+                    lhsT=x_codes[j][:, e * P:(e + 1) * P].bitcast(FP8X4),
+                    lhsT_scale=x_scales[j][:, e * P:(e + 1) * P],
+                    rhs=w_codes[h][:].bitcast(FP8X4),
+                    rhs_scale=w_scales[h][:],
+                    start=(what in "eo" or e == 0),
+                    stop=(what in "eo" or e == 1),
+                )
+            elif kind == "S":
+                dst, hbm = result(op[1], int(op[2]))
+                nc.sync.dma_start(out=hbm, in_=dst)
+            else:
+                what, j = op[1], int(op[2])
+                dst, hbm = result(what, j)
+                acc = psum_of[op[1:3]]
+                if what in "eo" and on_vector:
+                    nc.vector.tensor_copy(out=dst, in_=acc[:])
+                elif what in "eo":
+                    nc.scalar.copy(out=dst, in_=acc[:])
+                elif on_vector:
+                    nc.vector.tensor_scalar(out=dst, in0=acc[:], scalar1=0.5, scalar2=None, op0=MULT)
+                else:
+                    nc.scalar.activation(out=dst, in_=acc[:], func=COPY, scale=0.5)
+
+        queues = [TENSOR, VECTOR, SCALAR, GPSIMD, SYNC]
+        at = [0, 0, 0, 0, 0]
+        written = set()
+        last_dummy = [op for op in TENSOR if op[0] == "D"][-1]
+        while sum(at) < sum([len(q) for q in queues]):
+            before = sum(at)
+            for i in range(5):
+                while at[i] < len(queues[i]):
+                    op = queues[i][at[i]]
+                    if not all([n in written for n in needs(op)]):
+                        break
+                    key = {"T": "t" + op[1], "D": "d", "P": op[1:3]}.get(op[0])
+                    if key is not None and key not in psum_of:
+                        if len(opened) >= BANKS and opened[len(opened) - BANKS] not in emptied:
+                            break
+                        psum_of[key] = ps.tile([P, D], F32, name="bank%d" % (len(opened) % BANKS))
+                        opened.append(key)
+                    emit(op, queues[i])
+                    written.add(op)
+                    at[i] += 1
+                    if op[0] == "X":
+                        emptied.add("t" + op[1])
+                    elif op[0] == "E":
+                        emptied.add(op[1:3])
+                    elif op == last_dummy:
+                        emptied.add("d")
+            assert sum(at) > before, "the queues block each other"

@@ -67,8 +67,8 @@ def tile_ammattention_pa_kernel(tc, x_bytes, x_scale, w_kv, out_0, out_1, out_2)
 
         scale4 = sb.tile([P, 4], F32, name="scale4")
         nc.scalar.dma_start(out=scale4[:], in_=x_scale.rearrange("a b (p t) -> p (a b t)", t=4))
-        x_raw = [sb.tile([P, 2, D], U8, name="x_raw%d" % j) for j in range(GROUPS)]
-        w_raw = [sb.tile([P, 4, D], BF16, name="w_raw%d" % h) for h in range(2)]
+        x_raw = [sb.tile([P, 2, D], U8, name="x_raw%d" % j, align_bytes=256) for j in range(GROUPS)]
+        w_raw = [sb.tile([P, 4, D], BF16, name="w_raw%d" % h, align_bytes=256) for h in range(2)]
         nc.sync.dma_start(out=x_raw[0][:], in_=x_view[:, 0])
         for c0 in (0, D // 2):
             nc.sync.dma_start(out=w_raw[1][:, :, c0:c0 + D // 2], in_=w_view[:, :, D + c0:D + c0 + D // 2])
@@ -92,9 +92,9 @@ def tile_ammattention_pa_kernel(tc, x_bytes, x_scale, w_kv, out_0, out_1, out_2)
         w_grp = [sb.tile([P, D, 4], BF16, name="w_grp%d" % h, align_bytes=64) for h in range(2)]
         w_codes = [sb.tile([P, D], U32, name="w_codes%d" % h, align_bytes=64) for h in range(2)]
         w_scales = [sb.tile([P, D], U8, name="w_scales%d" % h, align_bytes=64) for h in range(2)]
-        v_sb = [sb.tile([P, 2, D], F32, name="v_sb%d" % j) for j in range(GROUPS)]
-        kl_sb = [sb.tile([P, D], F32, name="kl_sb%d" % j) for j in range(GROUPS)]
-        vl_sb = [sb.tile([P, D], F32, name="vl_sb%d" % j) for j in range(GROUPS)]
+        v_sb = [sb.tile([P, 2, D], F32, name="v_sb%d" % j, align_bytes=256) for j in range(GROUPS)]
+        kl_sb = [sb.tile([P, D], F32, name="kl_sb%d" % j, align_bytes=256) for j in range(GROUPS)]
+        vl_sb = [sb.tile([P, D], F32, name="vl_sb%d" % j, align_bytes=256) for j in range(GROUPS)]
 
         opened = []
         emptied = set()

@@ -21,16 +21,16 @@ CHUNK = 128
 BANKS = 8
 
 VECTOR = "C01 W10 W12 X0 R1 Q0 X1 Ee0 Q1 X2 C30 Q2 R0 X3 Ek0 Q3 Ee3 Eo3 El3".split()
-SCALAR = "C00 W11 W13 C10 C11 W02 W00 W01 W03 Eo0 El0 Eo1 Ee1 El1 Eo2 Ee2 El2 Ek1 Ek2 Ek3".split()
-TENSOR = "T01 T00 D1 D2 T10 T11 Pe0 Pl00 Po0 Pl01 T21 T20 D0 Po1 Pl10 Pe1 Pl11 T31 T30 Po2 Pe2 Pk00 Pk01 Pl20 Pl21 Pk10 Pk11 Pk20 Pk21 Pe3 Pl30 Po3 Pk30 Pl31 Pk31".split()
-GPSIMD = "C21 C20 C31".split()
+SCALAR = "C00 W11 W13 C10 C11 C20 W02 W00 W01 W03 Eo0 El0 Eo1 Ee1 El1 Eo2 Ee2 El2 Ek1 Ek2 Ek3".split()
+TENSOR = "T01 T00 D1 D2 T10 T11 T21 T20 Pe0 Pl00 Po0 Pl01 Po1 Pl10 Pe1 Pl11 T31 T30 Po2 Pe2 Pk00 Pk01 Pl20 Pl21 Pk10 Pk11 Pk20 Pk21 Pe3 Pl30 Po3 Pk30 Pl31 Pk31".split()
+GPSIMD = "C21 C31".split()
 SYNC = "Se0 So0 Sl0 So1 Se1 Sl1 So2 Se2 Sk0 Sl2 Sk1 Sk2 Se3 So3 Sl3 Sk3".split()
 
 
 def needs(op):
     kind, a = op[0], op[1]
     if kind == "C":
-        return ["Q" + str(int(a) - 2)] if int(a) >= 2 else []
+        return {"2": ["W10", "W11", "W12", "W13"], "3": ["Q1"]}.get(a, [])
     if kind == "T":
         return ["C" + op[1:]]
     if kind == "X":
@@ -115,7 +115,10 @@ def tile_ammattention_pa_kernel(tc, x_bytes, x_scale, w_kv, out_0, out_1, out_2)
             if kind == "C":
                 j, e = int(op[1]), int(op[2])
                 if j not in x_bf:
-                    x_bf[j] = sb.tile([P, 2, D], BF16, name=("x_bf%d" % j) if j < 2 else ("x_grp%d" % (j - 2)), align_bytes=64)
+                    if j == 2:
+                        x_bf[j] = sb.tile([P, 2, D], BF16, name="w_raw1", align_bytes=256)
+                    else:
+                        x_bf[j] = sb.tile([P, 2, D], BF16, name=("x_bf%d" % j) if j < 2 else "x_grp1", align_bytes=64)
                 if on_vector:
                     nc.vector.tensor_copy(out=x_bf[j][:, e, :], in_=x_raw[j][:, e, :].bitcast(FP8))
                 elif queue is GPSIMD:

from contextlib import ExitStack

import concourse.mybir as mybir
from concourse.masks import make_identity

FLOPS = 2 * 1024 * 512 * 1024

F32 = mybir.dt.float32
BF16 = mybir.dt.bfloat16
U32 = mybir.dt.uint32
U8 = mybir.dt.uint8
FP8 = mybir.dt.float8_e4m3fn
FP8X4 = mybir.dt.float8_e4m3fn_x4
MULT = mybir.AluOpType.mult
COPY = mybir.ActivationFunctionType.Copy

P = 128
D = 512
GROUPS = 4
CHUNK = 128
BANKS = 8

VECTOR = "C01 W10 W12 X0 R1 Q0 X1 Ee0 Q1 X2 C30 Q2 R0 X3 Ek0 Q3 Ee3 Eo3 El3".split()
SCALAR = "C00 W11 W13 C10 C11 C20 W02 W00 W01 W03 Eo0 El0 Eo1 Ee1 El1 Eo2 Ee2 El2 Ek1 Ek2 Ek3".split()
TENSOR = "T01 T00 D1 D2 T10 T11 T21 T20 Pe0 Pl00 Po0 Pl01 Po1 Pl10 Pe1 Pl11 T31 T30 Po2 Pe2 Pk00 Pk01 Pl20 Pl21 Pk10 Pk11 Pk20 Pk21 Pe3 Pl30 Po3 Pk30 Pl31 Pk31".split()
GPSIMD = "C21 C31".split()
SYNC = "Se0 So0 Sl0 So1 Se1 Sl1 So2 Se2 Sk0 Sl2 Sk1 Sk2 Se3 So3 Sl3 Sk3".split()


def needs(op):
    kind, a = op[0], op[1]
    if kind == "C":
        return {"2": ["W10", "W11", "W12", "W13"], "3": ["Q1"]}.get(a, [])
    if kind == "T":
        return ["C" + op[1:]]
    if kind == "X":
        return ["T" + a + "0", "T" + a + "1"]
    if kind == "Q":
        return ["X" + a]
    if kind == "R":
        return ["W" + a + str(c) for c in range(D // CHUNK)]
    if kind == "D":
        return ["W1" + a]
    if kind == "P":
        j = op[2]
        first = ["P" + a + j + "0"] if op[3:] == "1" else []
        return ["Q" + j, "R0" if a == "k" else "R1"] + first
    if kind == "E":
        return ["P" + op[1:] + ("1" if a in "lk" else "")]
    if kind == "S":
        return ["E" + op[1:]]
    return []


def tile_ammattention_pa_kernel(tc, x_bytes, x_scale, w_kv, out_0, out_1, out_2):
    nc = tc.nc
    x_view = x_bytes.rearrange("o (j m e) k -> m (o j) e k", j=GROUPS, m=P, e=2)
    w_view = w_kv.rearrange("(p t) n -> p t n", t=4)
    v_view = out_0.rearrange("o (j m e) n -> m (o j) e n", j=GROUPS, m=P, e=2)
    kl_view = out_1.rearrange("o (j m) n -> m (o j) n", j=GROUPS, m=P)
    vl_view = out_2.rearrange("o (j m) n -> m (o j) n", j=GROUPS, m=P)

    with ExitStack() as ctx:
        sb = ctx.enter_context(tc.tile_pool(name="sb", bufs=1))
        ps = ctx.enter_context(tc.psum_pool(name="ps", bufs=1))
        ctx.enter_context(tc.manual_schedule())

        scale4 = sb.tile([P, 4], F32, name="scale4")
        nc.scalar.dma_start(out=scale4[:], in_=x_scale.rearrange("a b (p t) -> p (a b t)", t=4))
        x_raw = [sb.tile([P, 2, D], U8, name="x_raw%d" % j, align_bytes=256) for j in range(GROUPS)]
        w_raw = [sb.tile([P, 4, D], BF16, name="w_raw%d" % h, align_bytes=256) for h in range(2)]
        nc.sync.dma_start(out=x_raw[0][:], in_=x_view[:, 0])
        for c0 in (0, D // 2):
            nc.sync.dma_start(out=w_raw[1][:, :, c0:c0 + D // 2], in_=w_view[:, :, D + c0:D + c0 + D // 2])
        for j in range(1, GROUPS):
            nc.sync.dma_start(out=x_raw[j][:], in_=x_view[:, j])
        nc.sync.dma_start(out=w_raw[0][:], in_=w_view[:, :, 0:D])

        zeros = sb.tile([P, P], BF16, name="zeros")
        nc.gpsimd.memset(zeros[:], 0.0)
        ident = sb.tile([P, P], F32, name="ident")
        make_identity(nc, ident[:])
        one_col = sb.tile([P, 1], F32, name="one_col")
        one_out = sb.tile([P, 1], F32, name="one_out")
        nc.vector.memset(one_col[:], 0.0)
        nc.scalar.activation(out=one_out[:], in_=one_col[:], func=COPY, scale=0.5)

        x_grp = [sb.tile([P, 2 * P, 4], BF16, name="x_grp%d" % j, align_bytes=64) for j in range(GROUPS)]
        x_bf = {}
        x_codes = [sb.tile([P, 2 * P], U32, name="x_codes%d" % j, align_bytes=64) for j in range(GROUPS)]
        x_scales = [sb.tile([P, 2 * P], U8, name="x_scales%d" % j, align_bytes=64) for j in range(GROUPS)]
        w_grp = [sb.tile([P, D, 4], BF16, name="w_grp%d" % h, align_bytes=64) for h in range(2)]
        w_codes = [sb.tile([P, D], U32, name="w_codes%d" % h, align_bytes=64) for h in range(2)]
        w_scales = [sb.tile([P, D], U8, name="w_scales%d" % h, align_bytes=64) for h in range(2)]
        v_sb = [sb.tile([P, 2, D], F32, name="v_sb%d" % j, align_bytes=256) for j in range(GROUPS)]
        kl_sb = [sb.tile([P, D], F32, name="kl_sb%d" % j, align_bytes=256) for j in range(GROUPS)]
        vl_sb = [sb.tile([P, D], F32, name="vl_sb%d" % j, align_bytes=256) for j in range(GROUPS)]

        opened = []
        emptied = set()
        psum_of = {}

        def result(what, j):
            if what == "e":
                return v_sb[j][:, 0, :], v_view[:, j, 0, :]
            if what == "o":
                return v_sb[j][:, 1, :], v_view[:, j, 1, :]
            if what == "l":
                return vl_sb[j][:], vl_view[:, j]
            return kl_sb[j][:], kl_view[:, j]

        def emit(op, queue):
            kind = op[0]
            on_vector = queue is VECTOR
            if kind == "C":
                j, e = int(op[1]), int(op[2])
                if j not in x_bf:
                    if j == 2:
                        x_bf[j] = sb.tile([P, 2, D], BF16, name="w_raw1", align_bytes=256)
                    else:
                        x_bf[j] = sb.tile([P, 2, D], BF16, name=("x_bf%d" % j) if j < 2 else "x_grp1", align_bytes=64)
                if on_vector:
                    nc.vector.tensor_copy(out=x_bf[j][:, e, :], in_=x_raw[j][:, e, :].bitcast(FP8))
                elif queue is GPSIMD:
                    nc.gpsimd.tensor_copy(out=x_bf[j][:, e, :], in_=x_raw[j][:, e, :].bitcast(FP8))
                else:
                    nc.scalar.copy(out=x_bf[j][:, e, :], in_=x_raw[j][:, e, :].bitcast(FP8))
            elif kind == "T":
                j, e = int(op[1]), int(op[2])
                words = x_bf[j][:, e, :].bitcast(F32)
                for u in range(2):
                    nc.tensor.transpose(psum_of["t" + op[1]][:, u * 2 * P + e * P:u * 2 * P + (e + 1) * P], words[:, u:2 * P:2], ident[:])
            elif kind == "X":
                j = int(op[1])
                nc.vector.tensor_tensor(
                    out=x_grp[j][:].rearrange("p c (u i) -> p c u i", u=2),
                    in0=psum_of["t" + op[1]][:].bitcast(BF16).rearrange("p (u c i) -> p c u i", u=2, i=2),
                    in1=scale4[:].rearrange("p (u i) -> p u i", u=2).unsqueeze(1).to_broadcast([P, 2 * P, 2, 2]),
                    op=MULT,
                )
            elif kind == "Q":
                j = int(op[1])
                nc.vector.quantize_mx(out=x_codes[j][:].bitcast(FP8X4), scales=x_scales[j][:], in_=x_grp[j][:].rearrange("p c t -> p (c t)"))
            elif kind == "W":
                h, c0 = int(op[1]), int(op[2]) * CHUNK
                src = w_raw[h][:, :, c0:c0 + CHUNK].rearrange("p t (c i) -> p c t i", i=4)
                dst = w_grp[h][:, c0:c0 + CHUNK, :].rearrange("p (c i) t -> p c t i", i=4)
                if on_vector:
                    nc.vector.tensor_copy(out=dst, in_=src)
                else:
                    nc.scalar.copy(out=dst, in_=src)
            elif kind == "R":
                h = int(op[1])
                nc.vector.quantize_mx(out=w_codes[h][:].bitcast(FP8X4), scales=w_scales[h][:], in_=w_grp[h][:].rearrange("p n t -> p (n t)"))
            elif kind == "D":
                c0 = int(op[1]) * CHUNK
                nc.tensor.matmul(out=psum_of["d"][:], lhsT=zeros[:], rhs=w_grp[1][:, c0:c0 + CHUNK, :].rearrange("p n t -> p (n t)"), start=True, stop=True)
            elif kind == "P":
                what, j = op[1], int(op[2])
                e = {"e": 0, "o": 1}.get(what, int(op[3:] or 0))
                h = 0 if what == "k" else 1
                nc.tensor.matmul_mx(
                    out=psum_of[op[1:3]][:],
                    lhsT=x_codes[j][:, e * P:(e + 1) * P].bitcast(FP8X4),
                    lhsT_scale=x_scales[j][:, e * P:(e + 1) * P],
                    rhs=w_codes[h][:].bitcast(FP8X4),
                    rhs_scale=w_scales[h][:],
                    start=(what in "eo" or e == 0),
                    stop=(what in "eo" or e == 1),
                )
            elif kind == "S":
                dst, hbm = result(op[1], int(op[2]))
                nc.sync.dma_start(out=hbm, in_=dst)
            else:
                what, j = op[1], int(op[2])
                dst, hbm = result(what, j)
                acc = psum_of[op[1:3]]
                if what in "eo" and on_vector:
                    nc.vector.tensor_copy(out=dst, in_=acc[:])
                elif what in "eo":
                    nc.scalar.copy(out=dst, in_=acc[:])
                elif on_vector:
                    nc.vector.tensor_scalar(out=dst, in0=acc[:], scalar1=0.5, scalar2=None, op0=MULT)
                else:
                    nc.scalar.activation(out=dst, in_=acc[:], func=COPY, scale=0.5)

        queues = [TENSOR, VECTOR, SCALAR, GPSIMD, SYNC]
        at = [0, 0, 0, 0, 0]
        written = set()
        last_dummy = [op for op in TENSOR if op[0] == "D"][-1]
        while sum(at) < sum([len(q) for q in queues]):
            before = sum(at)
            for i in range(5):
                while at[i] < len(queues[i]):
                    op = queues[i][at[i]]
                    if not all([n in written for n in needs(op)]):
                        break
                    key = {"T": "t" + op[1], "D": "d", "P": op[1:3]}.get(op[0])
                    if key is not None and key not in psum_of:
                        if len(opened) >= BANKS and opened[len(opened) - BANKS] not in emptied:
                            break
                        psum_of[key] = ps.tile([P, D], F32, name="bank%d" % (len(opened) % BANKS))
                        opened.append(key)
                    emit(op, queues[i])
                    written.add(op)
                    at[i] += 1
                    if op[0] == "X":
                        emptied.add("t" + op[1])
                    elif op[0] == "E":
                        emptied.add(op[1:3])
                    elif op == last_dummy:
                        emptied.add("d")
            assert sum(at) > before, "the queues block each other"
